import numpy as np
import ml_dtypes


def mxq(x, axis, fmt="e4m3"):
    dtype, down = {"e4m3": (ml_dtypes.float8_e4m3fn, 7), "e5m2": (ml_dtypes.float8_e5m2, 14)}[fmt]
    v = np.moveaxis(np.asarray(x, np.float32).astype(ml_dtypes.bfloat16).astype(np.float64), axis, -1)
    blocks = v.reshape(v.shape[:-1] + (-1, 32))
    amax = np.abs(blocks).max(-1, keepdims=True)
    byte = np.maximum(np.where(amax > 0, np.frexp(amax)[1] - 1 + 127, 0) - down, 1)
    scale = np.exp2(byte - 127.0)
    codes = (blocks / scale).astype(np.float32).astype(dtype).astype(np.float64)
    return np.moveaxis((codes * scale).reshape(v.shape), -1, axis)


WIDE = False


def mx_kscale(k):
    if not WIDE:
        return np.ones(k)
    levels = np.array([10, -10, 5, -5, 0])
    a = np.random.permutation(np.resize(levels, k // 512 * 4)).reshape(k // 512, 4)
    idx = np.arange(k)
    return np.exp2(a[idx // 512, idx % 128 // 32])


BF16 = ml_dtypes.bfloat16


def bf(x):
    return np.asarray(x, np.float32).astype(BF16)


def f64(x):
    return np.asarray(x).astype(np.float64)


B, S, H, NH, HD = 1, 512, 8192, 16, 32
E = NH * HD


def heads(t):
    return t.reshape(B, S, NH, HD).transpose(0, 2, 1, 3)


def setup_inputs():
    s = mx_kscale(H)
    c = S ** -0.25
    return {"hidden_states": bf(np.random.standard_normal((B, S, H)) * s),
            "Wk": bf(np.random.standard_normal((H, E)) * c / np.sqrt(H) / s[:, None]),
            "bk": bf(np.random.standard_normal(E) / np.sqrt(S)),
            "Wv": bf(np.random.standard_normal((H, E)) * c / np.sqrt(H) / s[:, None]),
            "bv": bf(np.random.standard_normal(E) / np.sqrt(S))}


def reference(hidden_states, Wk, bk, Wv, bv):
    xq = mxq(f64(hidden_states), 2, "e4m3")
    k = heads((xq @ mxq(f64(Wk), 0, "e4m3")) + f64(bk))
    v = heads((xq @ mxq(f64(Wv), 0, "e4m3")) + f64(bv))
    return mxq(k, 2, "e4m3").transpose(0, 1, 3, 2) @ mxq(v, 2, "e4m3")

@@ -1,0 +1,172 @@
+from contextlib import ExitStack
+
+import concourse.mybir as mybir
+from concourse.masks import make_identity
+
+F32 = mybir.dt.float32
+BF16 = mybir.dt.bfloat16
+U32 = mybir.dt.uint32
+U8 = mybir.dt.uint8
+FP8X4 = mybir.dt.float8_e4m3fn_x4
+ADD = mybir.AluOpType.add
+
+P = 128
+PACK = 4
+K_PASS = P * PACK
+S = 512
+H = 8192
+E = 512
+HEAD = 32
+PASSES = H // K_PASS
+HEADS_PER_TILE = P // HEAD
+COL_TILES = E // P
+X_PIECE = 4096
+PASSES_PER_W_LOAD = 2
+RUN = 4
+VECTOR_COLS = E // 2
+
+FLOPS = 2 * S * H * 2 * E + 2 * (E // HEAD) * HEAD * HEAD * S
+
+
+def regroup(nc, grouped, rows):
+    dst = grouped.rearrange("p (c i) t -> p c t i", i=RUN)
+    src = rows.rearrange("p t (c i) -> p c t i", i=RUN)
+    cut = VECTOR_COLS // RUN
+    nc.vector.tensor_copy(out=dst[:, :cut], in_=src[:, :cut])
+    nc.scalar.copy(out=dst[:, cut:], in_=src[:, cut:])
+
+
+def quantise_columns(nc, grouped, codes, scales):
+    flat = grouped.rearrange("p n t -> p (n t)")
+    for first, last in ((0, VECTOR_COLS), (VECTOR_COLS, E)):
+        nc.vector.quantize_mx(
+            out=codes[:, first:last].bitcast(FP8X4),
+            scales=scales[:, first:last],
+            in_=flat[:, first * PACK : last * PACK],
+        )
+
+
+def tile_linearattention_pa_k_kernel(tc, hidden_states, Wk, bk, Wv, bv, out):
+    nc = tc.nc
+    with ExitStack() as stack:
+        consts = stack.enter_context(tc.tile_pool(name="consts", bufs=1))
+        keep = stack.enter_context(tc.tile_pool(name="keep", bufs=1))
+        raw = stack.enter_context(tc.tile_pool(name="raw", bufs=10))
+        x_stage = stack.enter_context(tc.tile_pool(name="x_stage", bufs=3))
+        w_stage = stack.enter_context(tc.tile_pool(name="w_stage", bufs=4))
+        kv_stage = stack.enter_context(tc.tile_pool(name="kv_stage", bufs=2))
+        psum = stack.enter_context(tc.psum_pool(name="psum", bufs=8))
+
+        ident = consts.tile([P, P], F32)
+        make_identity(nc, ident[:])
+
+        ones = consts.tile([P, P], BF16)
+        nc.vector.memset(ones[:], 1.0)
+        bias_rows = consts.tile([P, 2, E], BF16)
+        nc.vector.memset(bias_rows[:], 0.0)
+        nc.scalar.dma_start(out=bias_rows[0:1, 0, :], in_=bk.rearrange("(o e) -> o e", o=1))
+        nc.scalar.dma_start(out=bias_rows[0:1, 1, :], in_=bv.rearrange("(o e) -> o e", o=1))
+        bias = consts.tile([P, 2, E], F32)
+        for m in range(2):
+            spread = psum.tile([P, E], F32, tag="bank")
+            nc.tensor.matmul(
+                out=spread[:], lhsT=ones[:], rhs=bias_rows[:, m, :], start=True, stop=True
+            )
+            nc.vector.tensor_copy(out=bias[:, m, :], in_=spread[:])
+
+        x_rows = hidden_states.flatten_outer_dims().rearrange("(p t) k -> p t k", t=PACK)
+        x_codes = keep.tile([P, PACK, PASSES * P], U32, align_bytes=64)
+        x_scales = keep.tile([P, PACK, PASSES * P], U8, align_bytes=64)
+        banks_done = 0
+        for t in range(PACK):
+            for piece in range(H // X_PIECE):
+                x_raw = raw.tile([P, X_PIECE], BF16, tag="raw")
+                nc.sync.dma_start(
+                    out=x_raw[:], in_=x_rows[:, t, piece * X_PIECE : (piece + 1) * X_PIECE]
+                )
+                x_words = x_raw[:].bitcast(F32)
+                for quad in range(X_PIECE // (4 * K_PASS)):
+                    x_grouped = x_stage.tile([P, 4 * P * PACK], BF16, align_bytes=64)
+                    grouped_words = x_grouped[:].bitcast(F32).rearrange(
+                        "p (g s u) -> p g s u", g=4, u=2
+                    )
+                    for pair in range(2):
+                        xt = psum.tile([P, 2, 2, P], F32, tag="bank")
+                        for g in range(2):
+                            for u in range(2):
+                                first = (((quad * 2 + pair) * 2 + g) * 2 + u) * P
+                                nc.tensor.transpose(
+                                    xt[:, g, u, :], x_words[:, first : first + P], ident[:]
+                                )
+                        words_out = grouped_words[:, 2 * pair : 2 * pair + 2]
+                        words_in = xt[:].rearrange("p g u s -> p g s u")
+                        if banks_done % 4 == 3:
+                            nc.vector.tensor_copy(out=words_out, in_=words_in)
+                        else:
+                            nc.scalar.copy(out=words_out, in_=words_in)
+                        banks_done += 1
+                    first_col = (piece * (X_PIECE // K_PASS) + quad * 4) * P
+                    nc.vector.quantize_mx(
+                        out=x_codes[:, t, first_col : first_col + 4 * P].bitcast(FP8X4),
+                        scales=x_scales[:, t, first_col : first_col + 4 * P],
+                        in_=x_grouped[:],
+                    )
+
+        kv_codes = []
+        kv_scales = []
+        for m, weights in enumerate((Wk, Wv)):
+            w_rows = weights.rearrange("(c q e) n -> q c (e n)", q=P, e=2)
+            acc = [psum.tile([P, E], F32, tag="bank", name="acc%d_%d" % (m, t)) for t in range(PACK)]
+            for load in range(PASSES // PASSES_PER_W_LOAD):
+                w_raw = raw.tile([P, PASSES_PER_W_LOAD, PACK, E], BF16, tag="raw")
+                nc.sync.dma_start(
+                    out=w_raw[:].rearrange("p g (u e) n -> p (g u) (e n)", e=2),
+                    in_=w_rows[:, 2 * PASSES_PER_W_LOAD * load : 2 * PASSES_PER_W_LOAD * (load + 1), :],
+                )
+                for i in range(PASSES_PER_W_LOAD):
+                    g = load * PASSES_PER_W_LOAD + i
+                    w_grouped = w_stage.tile([P, E, PACK], BF16, tag="grouped", align_bytes=64)
+                    regroup(nc, w_grouped[:], w_raw[:, i])
+                    w_codes = w_stage.tile([P, E], U32, align_bytes=64)
+                    w_scales = w_stage.tile([P, E], U8, align_bytes=64)
+                    quantise_columns(nc, w_grouped[:], w_codes, w_scales)
+                    for t in range(PACK):
+                        nc.tensor.matmul_mx(
+                            out=acc[t][:],
+                            lhsT=x_codes[:, t, g * P : (g + 1) * P].bitcast(FP8X4),
+                            lhsT_scale=x_scales[:, t, g * P : (g + 1) * P],
+                            rhs=w_codes[:].bitcast(FP8X4),
+                            rhs_scale=w_scales[:],
+                            start=(g == 0),
+                            stop=(g == PASSES - 1),
+                        )
+            rounded = kv_stage.tile([P, PACK, E], BF16)
+            for t in range(PACK):
+                nc.vector.tensor_tensor(out=rounded[:, t, :], in0=acc[t][:], in1=bias[:, m, :], op=ADD)
+            grouped = w_stage.tile([P, E, PACK], BF16, tag="grouped", align_bytes=64)
+            regroup(nc, grouped[:], rounded[:])
+            codes = keep.tile([P, E], U32, name="codes%d" % m, align_bytes=64)
+            scales = keep.tile([P, E], U8, name="scales%d" % m, align_bytes=64)
+            quantise_columns(nc, grouped[:], codes, scales)
+            kv_codes.append(codes)
+            kv_scales.append(scales)
+
+        products = psum.tile([P, COL_TILES, HEADS_PER_TILE, HEAD], F32, tag="bank")
+        for c in range(COL_TILES):
+            cols = slice(c * P, (c + 1) * P)
+            nc.tensor.matmul_mx(
+                out=products[:, c].rearrange("p r e -> p (r e)"),
+                lhsT=kv_codes[0][:, cols].bitcast(FP8X4),
+                lhsT_scale=kv_scales[0][:, cols],
+                rhs=kv_codes[1][:, cols].bitcast(FP8X4),
+                rhs_scale=kv_scales[1][:, cols],
+                start=True,
+                stop=True,
+            )
+        state = keep.tile([P, COL_TILES, HEAD], F32)
+        for r in range(HEADS_PER_TILE):
+            rows = slice(r * HEAD, (r + 1) * HEAD)
+            nc.vector.tensor_copy(out=state[rows, :, :], in_=products[rows, :, r, :])
+        nc.sync.dma_start(
+            out=out.flatten_outer_dims().rearrange("(c p) e -> p c e", p=P), in_=state[:]
+        )

@@ -21,9 +21,10 @@ PASSES = H // K_PASS
 HEADS_PER_TILE = P // HEAD
 COL_TILES = E // P
 X_PIECE = 4096
-PASSES_PER_W_LOAD = 2
+QUAD = 4
 RUN = 4
-VECTOR_COLS = E // 2
+VECTOR_COLS = 224
+K_STATE_LAG = 2
 
 FLOPS = 2 * S * H * 2 * E + 2 * (E // HEAD) * HEAD * HEAD * S
 
@@ -36,36 +37,73 @@ def regroup(nc, grouped, rows):
     nc.scalar.copy(out=dst[:, cut:], in_=src[:, cut:])
 
 
-def quantise_columns(nc, grouped, codes, scales):
-    flat = grouped.rearrange("p n t -> p (n t)")
-    for first, last in ((0, VECTOR_COLS), (VECTOR_COLS, E)):
-        nc.vector.quantize_mx(
-            out=codes[:, first:last].bitcast(FP8X4),
-            scales=scales[:, first:last],
-            in_=flat[:, first * PACK : last * PACK],
-        )
+def quantise(nc, grouped, codes, scales):
+    nc.vector.quantize_mx(out=codes.bitcast(FP8X4), scales=scales, in_=grouped)
 
 
 def tile_linearattention_pa_k_kernel(tc, hidden_states, Wk, bk, Wv, bv, out):
     nc = tc.nc
     with ExitStack() as stack:
+        stack.enter_context(tc.manual_schedule())
         consts = stack.enter_context(tc.tile_pool(name="consts", bufs=1))
         keep = stack.enter_context(tc.tile_pool(name="keep", bufs=1))
-        raw = stack.enter_context(tc.tile_pool(name="raw", bufs=10))
+        x_loads = stack.enter_context(tc.tile_pool(name="x_loads", bufs=5))
+        w_loads = stack.enter_context(tc.tile_pool(name="w_loads", bufs=14))
         x_stage = stack.enter_context(tc.tile_pool(name="x_stage", bufs=3))
         w_stage = stack.enter_context(tc.tile_pool(name="w_stage", bufs=4))
-        kv_stage = stack.enter_context(tc.tile_pool(name="kv_stage", bufs=2))
         psum = stack.enter_context(tc.psum_pool(name="psum", bufs=8))
 
         ident = consts.tile([P, P], F32)
         make_identity(nc, ident[:])
-
         ones = consts.tile([P, P], BF16)
         nc.vector.memset(ones[:], 1.0)
         bias_rows = consts.tile([P, 2, E], BF16)
         nc.vector.memset(bias_rows[:], 0.0)
         nc.scalar.dma_start(out=bias_rows[0:1, 0, :], in_=bk.rearrange("(o e) -> o e", o=1))
         nc.scalar.dma_start(out=bias_rows[0:1, 1, :], in_=bv.rearrange("(o e) -> o e", o=1))
+
+        x_rows = hidden_states.flatten_outer_dims().rearrange("(p t) k -> p t k", t=PACK)
+        x_codes = keep.tile([P, PACK, PASSES * P], U32, align_bytes=64)
+        x_scales = keep.tile([P, PACK, PASSES * P], U8, align_bytes=64)
+
+        def quantise_x(t, quad, x_grouped):
+            cols = slice(quad * QUAD * P, (quad + 1) * QUAD * P)
+            quantise(nc, x_grouped[:], x_codes[:, t, cols], x_scales[:, t, cols])
+
+        waiting = None
+        banks_done = 0
+        quads_per_piece = X_PIECE // (QUAD * K_PASS)
+        for t in range(PACK):
+            for quad in range(PASSES // QUAD):
+                if quad % quads_per_piece == 0:
+                    x_raw = x_loads.tile([P, X_PIECE], BF16)
+                    first_k = quad * QUAD * K_PASS
+                    nc.sync.dma_start(out=x_raw[:], in_=x_rows[:, t, first_k : first_k + X_PIECE])
+                    x_words = x_raw[:].bitcast(F32)
+                x_grouped = x_stage.tile([P, QUAD * P * PACK], BF16, align_bytes=64)
+                grouped_words = x_grouped[:].bitcast(F32).rearrange(
+                    "p (g s u) -> p g s u", g=QUAD, u=2
+                )
+                for pair in range(QUAD // 2):
+                    xt = psum.tile([P, 2, 2, P], F32, tag="bank")
+                    for g in range(2):
+                        for u in range(2):
+                            plane = (((quad % quads_per_piece) * 2 + pair) * 2 + g) * 2 + u
+                            nc.tensor.transpose(
+                                xt[:, g, u, :], x_words[:, plane * P : (plane + 1) * P], ident[:]
+                            )
+                    words_out = grouped_words[:, 2 * pair : 2 * pair + 2]
+                    words_in = xt[:].rearrange("p g u s -> p g s u")
+                    if banks_done % 4 == 3:
+                        nc.vector.tensor_copy(out=words_out, in_=words_in)
+                    else:
+                        nc.scalar.copy(out=words_out, in_=words_in)
+                    banks_done += 1
+                if waiting is not None:
+                    quantise_x(*waiting)
+                waiting = (t, quad, x_grouped)
+        quantise_x(*waiting)
+
         bias = consts.tile([P, 2, E], F32)
         for m in range(2):
             spread = psum.tile([P, E], F32, tag="bank")
@@ -74,82 +112,65 @@ def tile_linearattention_pa_k_kernel(tc, hidden_states, Wk, bk, Wv, bv, out):
             )
             nc.vector.tensor_copy(out=bias[:, m, :], in_=spread[:])
 
-        x_rows = hidden_states.flatten_outer_dims().rearrange("(p t) k -> p t k", t=PACK)
-        x_codes = keep.tile([P, PACK, PASSES * P], U32, align_bytes=64)
-        x_scales = keep.tile([P, PACK, PASSES * P], U8, align_bytes=64)
-        banks_done = 0
-        for t in range(PACK):
-            for piece in range(H // X_PIECE):
-                x_raw = raw.tile([P, X_PIECE], BF16, tag="raw")
-                nc.sync.dma_start(
-                    out=x_raw[:], in_=x_rows[:, t, piece * X_PIECE : (piece + 1) * X_PIECE]
-                )
-                x_words = x_raw[:].bitcast(F32)
-                for quad in range(X_PIECE // (4 * K_PASS)):
-                    x_grouped = x_stage.tile([P, 4 * P * PACK], BF16, align_bytes=64)
-                    grouped_words = x_grouped[:].bitcast(F32).rearrange(
-                        "p (g s u) -> p g s u", g=4, u=2
-                    )
-                    for pair in range(2):
-                        xt = psum.tile([P, 2, 2, P], F32, tag="bank")
-                        for g in range(2):
-                            for u in range(2):
-                                first = (((quad * 2 + pair) * 2 + g) * 2 + u) * P
-                                nc.tensor.transpose(
-                                    xt[:, g, u, :], x_words[:, first : first + P], ident[:]
-                                )
-                        words_out = grouped_words[:, 2 * pair : 2 * pair + 2]
-                        words_in = xt[:].rearrange("p g u s -> p g s u")
-                        if banks_done % 4 == 3:
-                            nc.vector.tensor_copy(out=words_out, in_=words_in)
-                        else:
-                            nc.scalar.copy(out=words_out, in_=words_in)
-                        banks_done += 1
-                    first_col = (piece * (X_PIECE // K_PASS) + quad * 4) * P
-                    nc.vector.quantize_mx(
-                        out=x_codes[:, t, first_col : first_col + 4 * P].bitcast(FP8X4),
-                        scales=x_scales[:, t, first_col : first_col + 4 * P],
-                        in_=x_grouped[:],
-                    )
+        sums = [
+            [psum.tile([P, E], F32, tag="bank", name="sums%d_%d" % (m, t)) for t in range(PACK)]
+            for m in range(2)
+        ]
+        kv_grouped = [
+            keep.tile([P, E, PACK], BF16, name="kv_grouped%d" % m, align_bytes=64) for m in range(2)
+        ]
+        kv_codes = [keep.tile([P, E], U32, name="kv_codes%d" % m, align_bytes=64) for m in range(2)]
+        kv_scales = [keep.tile([P, E], U8, name="kv_scales%d" % m, align_bytes=64) for m in range(2)]
 
-        kv_codes = []
-        kv_scales = []
+        def quantise_and_multiply(m, g, w_grouped):
+            w_codes = w_stage.tile([P, E], U32, align_bytes=64)
+            w_scales = w_stage.tile([P, E], U8, align_bytes=64)
+            quantise(nc, w_grouped[:].rearrange("p n t -> p (n t)"), w_codes[:], w_scales[:])
+            for t in range(PACK):
+                nc.tensor.matmul_mx(
+                    out=sums[m][t][:],
+                    lhsT=x_codes[:, t, g * P : (g + 1) * P].bitcast(FP8X4),
+                    lhsT_scale=x_scales[:, t, g * P : (g + 1) * P],
+                    rhs=w_codes[:].bitcast(FP8X4),
+                    rhs_scale=w_scales[:],
+                    start=(g == 0),
+                    stop=(g == PASSES - 1),
+                )
+
+        def add_bias_and_regroup(m):
+            rounded = keep.tile([P, PACK, E], BF16, name="rounded%d" % m)
+            for t in range(PACK):
+                nc.vector.tensor_tensor(
+                    out=rounded[:, t, :], in0=sums[m][t][:], in1=bias[:, m, :], op=ADD
+                )
+            regroup(nc, kv_grouped[m][:], rounded[:])
+
+        def quantise_kv(m):
+            quantise(
+                nc, kv_grouped[m][:].rearrange("p n t -> p (n t)"), kv_codes[m][:], kv_scales[m][:]
+            )
+
+        waiting = None
         for m, weights in enumerate((Wk, Wv)):
             w_rows = weights.rearrange("(c q e) n -> q c (e n)", q=P, e=2)
-            acc = [psum.tile([P, E], F32, tag="bank", name="acc%d_%d" % (m, t)) for t in range(PACK)]
-            for load in range(PASSES // PASSES_PER_W_LOAD):
-                w_raw = raw.tile([P, PASSES_PER_W_LOAD, PACK, E], BF16, tag="raw")
+            for g in range(PASSES):
+                w_raw = w_loads.tile([P, PACK, E], BF16)
                 nc.sync.dma_start(
-                    out=w_raw[:].rearrange("p g (u e) n -> p (g u) (e n)", e=2),
-                    in_=w_rows[:, 2 * PASSES_PER_W_LOAD * load : 2 * PASSES_PER_W_LOAD * (load + 1), :],
+                    out=w_raw[:].rearrange("p (u e) n -> p u (e n)", e=2),
+                    in_=w_rows[:, 2 * g : 2 * g + 2, :],
                 )
-                for i in range(PASSES_PER_W_LOAD):
-                    g = load * PASSES_PER_W_LOAD + i
-                    w_grouped = w_stage.tile([P, E, PACK], BF16, tag="grouped", align_bytes=64)
-                    regroup(nc, w_grouped[:], w_raw[:, i])
-                    w_codes = w_stage.tile([P, E], U32, align_bytes=64)
-                    w_scales = w_stage.tile([P, E], U8, align_bytes=64)
-                    quantise_columns(nc, w_grouped[:], w_codes, w_scales)
-                    for t in range(PACK):
-                        nc.tensor.matmul_mx(
-                            out=acc[t][:],
-                            lhsT=x_codes[:, t, g * P : (g + 1) * P].bitcast(FP8X4),
-                            lhsT_scale=x_scales[:, t, g * P : (g + 1) * P],
-                            rhs=w_codes[:].bitcast(FP8X4),
-                            rhs_scale=w_scales[:],
-                            start=(g == 0),
-                            stop=(g == PASSES - 1),
-                        )
-            rounded = kv_stage.tile([P, PACK, E], BF16)
-            for t in range(PACK):
-                nc.vector.tensor_tensor(out=rounded[:, t, :], in0=acc[t][:], in1=bias[:, m, :], op=ADD)
-            grouped = w_stage.tile([P, E, PACK], BF16, tag="grouped", align_bytes=64)
-            regroup(nc, grouped[:], rounded[:])
-            codes = keep.tile([P, E], U32, name="codes%d" % m, align_bytes=64)
-            scales = keep.tile([P, E], U8, name="scales%d" % m, align_bytes=64)
-            quantise_columns(nc, grouped[:], codes, scales)
-            kv_codes.append(codes)
-            kv_scales.append(scales)
+                w_grouped = w_stage.tile([P, E, PACK], BF16, align_bytes=64)
+                regroup(nc, w_grouped[:], w_raw[:])
+                if waiting is not None:
+                    quantise_and_multiply(*waiting)
+                waiting = (m, g, w_grouped)
+                if m == 1 and g == K_STATE_LAG:
+                    add_bias_and_regroup(0)
+                if m == 1 and g == K_STATE_LAG + 1:
+                    quantise_kv(0)
+        quantise_and_multiply(*waiting)
+        add_bias_and_regroup(1)
+        quantise_kv(1)
 
         products = psum.tile([P, COL_TILES, HEADS_PER_TILE, HEAD], F32, tag="bank")
         for c in range(COL_TILES):

@@ -23,16 +23,17 @@ COL_TILES = E // P
 X_PIECE = 4096
 QUAD = 4
 RUN = 4
-VECTOR_COLS = 224
+VECTOR_COLS = 240
+LAST_VECTOR_COLS = 352
 K_STATE_LAG = 2
 
 FLOPS = 2 * S * H * 2 * E + 2 * (E // HEAD) * HEAD * HEAD * S
 
 
-def regroup(nc, grouped, rows):
+def regroup(nc, grouped, rows, vector_cols):
     dst = grouped.rearrange("p (c i) t -> p c t i", i=RUN)
     src = rows.rearrange("p t (c i) -> p c t i", i=RUN)
-    cut = VECTOR_COLS // RUN
+    cut = vector_cols // RUN
     nc.vector.tensor_copy(out=dst[:, :cut], in_=src[:, :cut])
     nc.scalar.copy(out=dst[:, cut:], in_=src[:, cut:])
 
@@ -80,6 +81,7 @@ def tile_linearattention_pa_k_kernel(tc, hidden_states, Wk, bk, Wv, bv, out):
                     first_k = quad * QUAD * K_PASS
                     nc.sync.dma_start(out=x_raw[:], in_=x_rows[:, t, first_k : first_k + X_PIECE])
                     x_words = x_raw[:].bitcast(F32)
+                    words_per_pass = K_PASS // 2
                 x_grouped = x_stage.tile([P, QUAD * P * PACK], BF16, align_bytes=64)
                 grouped_words = x_grouped[:].bitcast(F32).rearrange(
                     "p (g s u) -> p g s u", g=QUAD, u=2
@@ -87,10 +89,12 @@ def tile_linearattention_pa_k_kernel(tc, hidden_states, Wk, bk, Wv, bv, out):
                 for pair in range(QUAD // 2):
                     xt = psum.tile([P, 2, 2, P], F32, tag="bank")
                     for g in range(2):
+                        first = (((quad % quads_per_piece) * 2 + pair) * 2 + g) * words_per_pass
                         for u in range(2):
-                            plane = (((quad % quads_per_piece) * 2 + pair) * 2 + g) * 2 + u
                             nc.tensor.transpose(
-                                xt[:, g, u, :], x_words[:, plane * P : (plane + 1) * P], ident[:]
+                                xt[:, g, u, :],
+                                x_words[:, first + u : first + words_per_pass : 2],
+                                ident[:],
                             )
                     words_out = grouped_words[:, 2 * pair : 2 * pair + 2]
                     words_in = xt[:].rearrange("p g u s -> p g s u")
@@ -137,13 +141,13 @@ def tile_linearattention_pa_k_kernel(tc, hidden_states, Wk, bk, Wv, bv, out):
                     stop=(g == PASSES - 1),
                 )
 
-        def add_bias_and_regroup(m):
+        def add_bias_and_regroup(m, vector_cols):
             rounded = keep.tile([P, PACK, E], BF16, name="rounded%d" % m)
             for t in range(PACK):
                 nc.vector.tensor_tensor(
                     out=rounded[:, t, :], in0=sums[m][t][:], in1=bias[:, m, :], op=ADD
                 )
-            regroup(nc, kv_grouped[m][:], rounded[:])
+            regroup(nc, kv_grouped[m][:], rounded[:], vector_cols)
 
         def quantise_kv(m):
             quantise(
@@ -152,24 +156,21 @@ def tile_linearattention_pa_k_kernel(tc, hidden_states, Wk, bk, Wv, bv, out):
 
         waiting = None
         for m, weights in enumerate((Wk, Wv)):
-            w_rows = weights.rearrange("(c q e) n -> q c (e n)", q=P, e=2)
+            w_rows = weights.rearrange("(g p t) n -> p g (t n)", p=P, t=PACK)
             for g in range(PASSES):
                 w_raw = w_loads.tile([P, PACK, E], BF16)
-                nc.sync.dma_start(
-                    out=w_raw[:].rearrange("p (u e) n -> p u (e n)", e=2),
-                    in_=w_rows[:, 2 * g : 2 * g + 2, :],
-                )
+                nc.sync.dma_start(out=w_raw[:].rearrange("p t n -> p (t n)"), in_=w_rows[:, g, :])
                 w_grouped = w_stage.tile([P, E, PACK], BF16, align_bytes=64)
-                regroup(nc, w_grouped[:], w_raw[:])
+                regroup(nc, w_grouped[:], w_raw[:], VECTOR_COLS)
                 if waiting is not None:
                     quantise_and_multiply(*waiting)
                 waiting = (m, g, w_grouped)
                 if m == 1 and g == K_STATE_LAG:
-                    add_bias_and_regroup(0)
+                    add_bias_and_regroup(0, VECTOR_COLS)
                 if m == 1 and g == K_STATE_LAG + 1:
                     quantise_kv(0)
         quantise_and_multiply(*waiting)
-        add_bias_and_regroup(1)
+        add_bias_and_regroup(1, LAST_VECTOR_COLS)
         quantise_kv(1)
 
         products = psum.tile([P, COL_TILES, HEADS_PER_TILE, HEAD], F32, tag="bank")

@@ -9,6 +9,7 @@ U32 = mybir.dt.uint32
 U8 = mybir.dt.uint8
 FP8X4 = mybir.dt.float8_e4m3fn_x4
 ADD = mybir.AluOpType.add
+IDENTITY = mybir.ActivationFunctionType.Identity
 
 P = 128
 PACK = 4
@@ -18,14 +19,16 @@ H = 8192
 E = 512
 HEAD = 32
 PASSES = H // K_PASS
-HEADS_PER_TILE = P // HEAD
+ROW_TILES = S // P
 COL_TILES = E // P
-X_PIECE = 4096
-QUAD = 4
+HEADS_PER_TILE = P // HEAD
+X_PIECES = (1, 1, 2, 2, 2, 2, 2, 2, 2)
+X_LEAD = 4
+LOAD_LEAD = 12
 RUN = 4
-VECTOR_COLS = 240
-LAST_VECTOR_COLS = 352
-K_STATE_LAG = 2
+MIXED_COLS = 304
+WEIGHT_COLS = 256
+LAST_COLS = 336
 
 FLOPS = 2 * S * H * 2 * E + 2 * (E // HEAD) * HEAD * HEAD * S
 
@@ -34,8 +37,8 @@ def regroup(nc, grouped, rows, vector_cols):
     dst = grouped.rearrange("p (c i) t -> p c t i", i=RUN)
     src = rows.rearrange("p t (c i) -> p c t i", i=RUN)
     cut = vector_cols // RUN
-    nc.vector.tensor_copy(out=dst[:, :cut], in_=src[:, :cut])
     nc.scalar.copy(out=dst[:, cut:], in_=src[:, cut:])
+    nc.vector.tensor_copy(out=dst[:, :cut], in_=src[:, :cut])
 
 
 def quantise(nc, grouped, codes, scales):
@@ -48,132 +51,231 @@ def tile_linearattention_pa_k_kernel(tc, hidden_states, Wk, bk, Wv, bv, out):
         stack.enter_context(tc.manual_schedule())
         consts = stack.enter_context(tc.tile_pool(name="consts", bufs=1))
         keep = stack.enter_context(tc.tile_pool(name="keep", bufs=1))
-        x_loads = stack.enter_context(tc.tile_pool(name="x_loads", bufs=5))
-        w_loads = stack.enter_context(tc.tile_pool(name="w_loads", bufs=14))
+        x_loads = stack.enter_context(tc.tile_pool(name="x_loads", bufs=6))
+        w_loads = stack.enter_context(tc.tile_pool(name="w_loads", bufs=12))
         x_stage = stack.enter_context(tc.tile_pool(name="x_stage", bufs=3))
         w_stage = stack.enter_context(tc.tile_pool(name="w_stage", bufs=4))
-        psum = stack.enter_context(tc.psum_pool(name="psum", bufs=8))
+        psum_k = stack.enter_context(tc.psum_pool(name="psum_k", bufs=4))
+        psum_x = stack.enter_context(tc.psum_pool(name="psum_x", bufs=4))
 
+        bias_rows = consts.tile([P, P], BF16)
+        nc.vector.memset(bias_rows[:], 0.0)
         ident = consts.tile([P, P], F32)
         make_identity(nc, ident[:])
-        ones = consts.tile([P, P], BF16)
-        nc.vector.memset(ones[:], 1.0)
-        bias_rows = consts.tile([P, 2, E], BF16)
-        nc.vector.memset(bias_rows[:], 0.0)
-        nc.scalar.dma_start(out=bias_rows[0:1, 0, :], in_=bk.rearrange("(o e) -> o e", o=1))
-        nc.scalar.dma_start(out=bias_rows[0:1, 1, :], in_=bv.rearrange("(o e) -> o e", o=1))
+        ident_cols = consts.tile([P, 2 * COL_TILES], BF16)
+        nc.vector.tensor_copy(out=ident_cols[:], in_=ident[:, : 2 * COL_TILES])
 
-        x_rows = hidden_states.flatten_outer_dims().rearrange("(p t) k -> p t k", t=PACK)
-        x_codes = keep.tile([P, PACK, PASSES * P], U32, align_bytes=64)
-        x_scales = keep.tile([P, PACK, PASSES * P], U8, align_bytes=64)
+        items = [("x", 0, g) for g in range(X_LEAD)]
+        for g in range(PASSES):
+            items.append(("w", 0, g))
+            if g + X_LEAD < PASSES:
+                items.append(("x", 0, g + X_LEAD))
+        first_v = len(items)
+        items += [("w", 1, g) for g in range(PASSES)]
 
-        def quantise_x(t, quad, x_grouped):
-            cols = slice(quad * QUAD * P, (quad + 1) * QUAD * P)
-            quantise(nc, x_grouped[:], x_codes[:, t, cols], x_scales[:, t, cols])
+        x_rows = hidden_states.flatten_outer_dims().rearrange("(r p) k -> p r k", p=P)
+        w_rows = [w.rearrange("(g p t) n -> p g (t n)", p=P, t=PACK) for w in (Wk, Wv)]
+        x_raw = {}
+        w_raw = {}
+        piece_at = {}
+        first = 0
+        for length in X_PIECES:
+            piece_at[first] = length
+            first += length
+        loads = [item for item in items if item[0] == "w" or item[2] in piece_at]
 
-        waiting = None
-        banks_done = 0
-        quads_per_piece = X_PIECE // (QUAD * K_PASS)
-        for t in range(PACK):
-            for quad in range(PASSES // QUAD):
-                if quad % quads_per_piece == 0:
-                    x_raw = x_loads.tile([P, X_PIECE], BF16)
-                    first_k = quad * QUAD * K_PASS
-                    nc.sync.dma_start(out=x_raw[:], in_=x_rows[:, t, first_k : first_k + X_PIECE])
-                    x_words = x_raw[:].bitcast(F32)
-                    words_per_pass = K_PASS // 2
-                x_grouped = x_stage.tile([P, QUAD * P * PACK], BF16, align_bytes=64)
-                grouped_words = x_grouped[:].bitcast(F32).rearrange(
-                    "p (g s u) -> p g s u", g=QUAD, u=2
+        def load(item):
+            kind, m, g = item
+            if kind == "x":
+                length = piece_at[g]
+                x_tile = x_loads.tile([P, ROW_TILES, max(X_PIECES) * K_PASS], BF16)
+                nc.sync.dma_start(
+                    out=x_tile[:, :, : length * K_PASS],
+                    in_=x_rows[:, :, g * K_PASS : (g + length) * K_PASS],
                 )
-                for pair in range(QUAD // 2):
-                    xt = psum.tile([P, 2, 2, P], F32, tag="bank")
-                    for g in range(2):
-                        first = (((quad % quads_per_piece) * 2 + pair) * 2 + g) * words_per_pass
-                        for u in range(2):
-                            nc.tensor.transpose(
-                                xt[:, g, u, :],
-                                x_words[:, first + u : first + words_per_pass : 2],
-                                ident[:],
-                            )
-                    words_out = grouped_words[:, 2 * pair : 2 * pair + 2]
-                    words_in = xt[:].rearrange("p g u s -> p g s u")
-                    if banks_done % 4 == 3:
-                        nc.vector.tensor_copy(out=words_out, in_=words_in)
-                    else:
-                        nc.scalar.copy(out=words_out, in_=words_in)
-                    banks_done += 1
-                if waiting is not None:
-                    quantise_x(*waiting)
-                waiting = (t, quad, x_grouped)
-        quantise_x(*waiting)
+                for i in range(length):
+                    x_raw[g + i] = (x_tile, i)
+            else:
+                w_tile = w_loads.tile([P, PACK, E], BF16)
+                nc.sync.dma_start(
+                    out=w_tile[:].rearrange("p t n -> p (t n)"), in_=w_rows[m][:, g, :]
+                )
+                w_raw[m, g] = w_tile
 
-        bias = consts.tile([P, 2, E], F32)
-        for m in range(2):
-            spread = psum.tile([P, E], F32, tag="bank")
-            nc.tensor.matmul(
-                out=spread[:], lhsT=ones[:], rhs=bias_rows[:, m, :], start=True, stop=True
-            )
-            nc.vector.tensor_copy(out=bias[:, m, :], in_=spread[:])
+        x_codes = keep.tile([P, PASSES, S], U32, align_bytes=64)
+        x_scales = keep.tile([P, PASSES, S], U8, align_bytes=64)
+        x_banks = {}
+        grouped = {}
 
-        sums = [
-            [psum.tile([P, E], F32, tag="bank", name="sums%d_%d" % (m, t)) for t in range(PACK)]
-            for m in range(2)
-        ]
-        kv_grouped = [
-            keep.tile([P, E, PACK], BF16, name="kv_grouped%d" % m, align_bytes=64) for m in range(2)
-        ]
-        kv_codes = [keep.tile([P, E], U32, name="kv_codes%d" % m, align_bytes=64) for m in range(2)]
-        kv_scales = [keep.tile([P, E], U8, name="kv_scales%d" % m, align_bytes=64) for m in range(2)]
+        def transpose_x(g):
+            x_tile, place = x_raw[g]
+            words_per_pass = K_PASS // 2
+            for half in range(2):
+                xt = psum_x.tile([P, 2, 2, P], F32, tag="bank")
+                for r in range(2):
+                    words = x_tile[:, 2 * half + r, :].bitcast(F32)
+                    for u in range(2):
+                        nc.tensor.transpose(
+                            xt[:, r, u, :],
+                            words[:, place * words_per_pass + u : (place + 1) * words_per_pass : 2],
+                            ident[:],
+                        )
+                x_banks[g, half] = xt
 
-        def quantise_and_multiply(m, g, w_grouped):
-            w_codes = w_stage.tile([P, E], U32, align_bytes=64)
-            w_scales = w_stage.tile([P, E], U8, align_bytes=64)
-            quantise(nc, w_grouped[:].rearrange("p n t -> p (n t)"), w_codes[:], w_scales[:])
-            for t in range(PACK):
+        def empty_x(g, share):
+            x_grouped = x_stage.tile([P, S * PACK], BF16, align_bytes=64)
+            words = x_grouped[:].bitcast(F32).rearrange("p (r s u) -> p r s u", r=ROW_TILES, u=2)
+            for half in range(2):
+                words_out = words[:, 2 * half : 2 * half + 2]
+                words_in = x_banks[g, half][:].rearrange("p r u s -> p r s u")
+                if half == 1 and share:
+                    nc.vector.tensor_copy(out=words_out, in_=words_in)
+                else:
+                    nc.scalar.copy(out=words_out, in_=words_in)
+            grouped["x", 0, g] = x_grouped
+
+        sums = {}
+        w_packed = {}
+
+        def regroup_w(m, g, vector_cols):
+            w_grouped = w_stage.tile([P, E, PACK], BF16, align_bytes=64)
+            regroup(nc, w_grouped[:], w_raw[m, g][:], vector_cols)
+            grouped["w", m, g] = w_grouped
+
+        def quantise_item(item):
+            kind, m, g = item
+            if kind == "x":
+                quantise(nc, grouped[item][:], x_codes[:, g, :], x_scales[:, g, :])
+            else:
+                w_codes = w_stage.tile([P, E], U32, align_bytes=64)
+                w_scales = w_stage.tile([P, E], U8, align_bytes=64)
+                flat = grouped[item][:].rearrange("p n t -> p (n t)")
+                quantise(nc, flat, w_codes[:], w_scales[:])
+                w_packed[m, g] = (w_codes, w_scales)
+
+        def multiply(m, g):
+            w_codes, w_scales = w_packed[m, g]
+            for c in range(COL_TILES):
+                if g == 0:
+                    pool = (psum_k, psum_x)[m]
+                    sums[m, c] = pool.tile([P, S], F32, tag="bank", name="sums%d_%d" % (m, c))
+                cols = slice(c * P, (c + 1) * P)
                 nc.tensor.matmul_mx(
-                    out=sums[m][t][:],
-                    lhsT=x_codes[:, t, g * P : (g + 1) * P].bitcast(FP8X4),
-                    lhsT_scale=x_scales[:, t, g * P : (g + 1) * P],
-                    rhs=w_codes[:].bitcast(FP8X4),
-                    rhs_scale=w_scales[:],
+                    out=sums[m, c][:],
+                    lhsT=w_codes[:, cols].bitcast(FP8X4),
+                    lhsT_scale=w_scales[:, cols],
+                    rhs=x_codes[:, g, :].bitcast(FP8X4),
+                    rhs_scale=x_scales[:, g, :],
                     start=(g == 0),
                     stop=(g == PASSES - 1),
                 )
 
-        def add_bias_and_regroup(m, vector_cols):
-            rounded = keep.tile([P, PACK, E], BF16, name="rounded%d" % m)
-            for t in range(PACK):
-                nc.vector.tensor_tensor(
-                    out=rounded[:, t, :], in0=sums[m][t][:], in1=bias[:, m, :], op=ADD
-                )
-            regroup(nc, kv_grouped[m][:], rounded[:], vector_cols)
+        bias = consts.tile([P, 2 * COL_TILES], F32)
+        rounded = [keep.tile([P, COL_TILES, S], BF16, name="rounded%d" % m) for m in range(2)]
+        kv_grouped = [
+            keep.tile([P, COL_TILES, P * PACK], BF16, name="kv_grouped%d" % m, align_bytes=64)
+            for m in range(2)
+        ]
+        kv_codes = [keep.tile([P, E], U32, name="kv_codes%d" % m, align_bytes=64) for m in range(2)]
+        kv_scales = [keep.tile([P, E], U8, name="kv_scales%d" % m, align_bytes=64) for m in range(2)]
+        kv_banks = {}
 
-        def quantise_kv(m):
-            quantise(
-                nc, kv_grouped[m][:].rearrange("p n t -> p (n t)"), kv_codes[m][:], kv_scales[m][:]
+        def spread_bias():
+            columns = psum_x.tile([P, 2 * COL_TILES], F32, tag="bank")
+            nc.tensor.matmul(
+                out=columns[:], lhsT=bias_rows[:], rhs=ident_cols[:], start=True, stop=True
             )
+            nc.vector.tensor_copy(out=bias[:], in_=columns[:])
 
-        waiting = None
-        for m, weights in enumerate((Wk, Wv)):
-            w_rows = weights.rearrange("(g p t) n -> p g (t n)", p=P, t=PACK)
-            for g in range(PASSES):
-                w_raw = w_loads.tile([P, PACK, E], BF16)
-                nc.sync.dma_start(out=w_raw[:].rearrange("p t n -> p (t n)"), in_=w_rows[:, g, :])
-                w_grouped = w_stage.tile([P, E, PACK], BF16, align_bytes=64)
-                regroup(nc, w_grouped[:], w_raw[:], VECTOR_COLS)
-                if waiting is not None:
-                    quantise_and_multiply(*waiting)
-                waiting = (m, g, w_grouped)
-                if m == 1 and g == K_STATE_LAG:
-                    add_bias_and_regroup(0, VECTOR_COLS)
-                if m == 1 and g == K_STATE_LAG + 1:
-                    quantise_kv(0)
-        quantise_and_multiply(*waiting)
-        add_bias_and_regroup(1, LAST_VECTOR_COLS)
-        quantise_kv(1)
+        def add_bias(m, c, on_vector):
+            column = bias[:, m * COL_TILES + c : m * COL_TILES + c + 1]
+            if on_vector:
+                nc.vector.tensor_scalar(
+                    out=rounded[m][:, c, :], in0=sums[m, c][:], scalar1=column, scalar2=None, op0=ADD
+                )
+            else:
+                nc.scalar.activation(
+                    out=rounded[m][:, c, :], in_=sums[m, c][:], func=IDENTITY, bias=column, scale=1.0
+                )
 
-        products = psum.tile([P, COL_TILES, HEADS_PER_TILE, HEAD], F32, tag="bank")
+        def transpose_kv(m, first_c, tiles):
+            turned = psum_k.tile([P, tiles, 2, P], F32, tag="bank")
+            for c in range(tiles):
+                words = rounded[m][:, first_c + c, :].bitcast(F32)
+                for u in range(2):
+                    nc.tensor.transpose(turned[:, c, u, :], words[:, u::2], ident[:])
+            kv_banks[m, first_c] = turned
+
+        def empty_kv(m, first_c, tiles, on_vector):
+            cols = slice(first_c, first_c + tiles)
+            words_out = kv_grouped[m][:, cols, :].bitcast(F32).rearrange(
+                "p c (n u) -> p c n u", u=2
+            )
+            words_in = kv_banks[m, first_c][:].rearrange("p c u n -> p c n u")
+            if on_vector:
+                nc.vector.tensor_copy(out=words_out, in_=words_in)
+            else:
+                nc.scalar.copy(out=words_out, in_=words_in)
+
+        def quantise_kv(m, first_c, tiles):
+            cols = slice(first_c * P, (first_c + tiles) * P)
+            flat = kv_grouped[m][:, first_c : first_c + tiles, :].rearrange("p c i -> p (c i)")
+            quantise(nc, flat, kv_codes[m][:, cols], kv_scales[m][:, cols])
+
+        for item in loads[:2]:
+            load(item)
+        for m, b in enumerate((bk, bv)):
+            nc.sync.dma_start(
+                out=bias_rows[m * COL_TILES : (m + 1) * COL_TILES, :],
+                in_=b.rearrange("(c p) -> c p", p=P),
+            )
+        for item in loads[2:LOAD_LEAD]:
+            load(item)
+        issued = LOAD_LEAD
+        transpose_x(0)
+
+        for j in range(len(items) + 2):
+            step = j - first_v
+            if j + 1 < len(items) and items[j + 1][0] == "x":
+                transpose_x(items[j + 1][2])
+            if j >= 2 and items[j - 2][0] == "w":
+                multiply(items[j - 2][1], items[j - 2][2])
+            if step in (5, 6):
+                transpose_kv(0, 2 * (step - 5), 2)
+            if j == X_LEAD:
+                spread_bias()
+            if j < len(items):
+                kind, m, g = items[j]
+                if kind == "x":
+                    empty_x(g, g < X_LEAD)
+                elif m == 0:
+                    regroup_w(m, g, MIXED_COLS)
+                elif g == PASSES - 1:
+                    regroup_w(m, g, LAST_COLS)
+                else:
+                    regroup_w(m, g, WEIGHT_COLS)
+                if items[j] in loads and issued < len(loads):
+                    load(loads[issued])
+                    issued += 1
+            if 2 <= step < 2 + COL_TILES:
+                add_bias(0, step - 2, False)
+            if step in (7, 8):
+                empty_kv(0, 2 * (step - 7), 2, False)
+            if 1 <= j <= len(items):
+                quantise_item(items[j - 1])
+            if step == 9:
+                quantise_kv(0, 0, COL_TILES)
+
+        for c in range(COL_TILES):
+            add_bias(1, c, c % 2 == 1)
+        for c in range(COL_TILES):
+            transpose_kv(1, c, 1)
+        for c in range(COL_TILES):
+            empty_kv(1, c, 1, c % 2 == 1)
+            if c >= 1:
+                quantise_kv(1, c - 1, 1)
+        quantise_kv(1, COL_TILES - 1, 1)
+        products = psum_k.tile([P, COL_TILES, HEADS_PER_TILE, HEAD], F32, tag="bank")
         for c in range(COL_TILES):
             cols = slice(c * P, (c + 1) * P)
             nc.tensor.matmul_mx(

@@ -25,7 +25,7 @@ HEADS_PER_TILE = P // HEAD
 X_PIECES = (1, 1, 2, 2, 2, 2, 2, 2, 2)
 X_LEAD = 4
 LOAD_LEAD = 12
-RUN = 4
+RUN = 8
 MIXED_COLS = 304
 WEIGHT_COLS = 256
 LAST_COLS = 336

@@ -23,8 +23,10 @@ ROW_TILES = S // P
 COL_TILES = E // P
 HEADS_PER_TILE = P // HEAD
 X_PIECES = (1, 1, 2, 2, 2, 2, 2, 2, 2)
+W_PIECE = 2
 X_LEAD = 4
-LOAD_LEAD = 12
+GROUP = 2
+LOAD_LEAD = 9
 RUN = 8
 MIXED_COLS = 304
 WEIGHT_COLS = 256
@@ -52,7 +54,7 @@ def tile_linearattention_pa_k_kernel(tc, hidden_states, Wk, bk, Wv, bv, out):
         consts = stack.enter_context(tc.tile_pool(name="consts", bufs=1))
         keep = stack.enter_context(tc.tile_pool(name="keep", bufs=1))
         x_loads = stack.enter_context(tc.tile_pool(name="x_loads", bufs=6))
-        w_loads = stack.enter_context(tc.tile_pool(name="w_loads", bufs=12))
+        w_loads = stack.enter_context(tc.tile_pool(name="w_loads", bufs=7))
         x_stage = stack.enter_context(tc.tile_pool(name="x_stage", bufs=3))
         w_stage = stack.enter_context(tc.tile_pool(name="w_stage", bufs=4))
         psum_k = stack.enter_context(tc.psum_pool(name="psum_k", bufs=4))
@@ -66,10 +68,9 @@ def tile_linearattention_pa_k_kernel(tc, hidden_states, Wk, bk, Wv, bv, out):
         nc.vector.tensor_copy(out=ident_cols[:], in_=ident[:, : 2 * COL_TILES])
 
         items = [("x", 0, g) for g in range(X_LEAD)]
-        for g in range(PASSES):
-            items.append(("w", 0, g))
-            if g + X_LEAD < PASSES:
-                items.append(("x", 0, g + X_LEAD))
+        for g in range(0, PASSES, GROUP):
+            items += [("w", 0, i) for i in range(g, g + GROUP)]
+            items += [("x", 0, i) for i in range(g + X_LEAD, min(g + X_LEAD + GROUP, PASSES))]
         first_v = len(items)
         items += [("w", 1, g) for g in range(PASSES)]
 
@@ -82,7 +83,11 @@ def tile_linearattention_pa_k_kernel(tc, hidden_states, Wk, bk, Wv, bv, out):
         for length in X_PIECES:
             piece_at[first] = length
             first += length
-        loads = [item for item in items if item[0] == "w" or item[2] in piece_at]
+        loads = [
+            item
+            for item in items
+            if (item[0] == "w" and item[2] % W_PIECE == 0) or (item[0] == "x" and item[2] in piece_at)
+        ]
 
         def load(item):
             kind, m, g = item
@@ -96,11 +101,13 @@ def tile_linearattention_pa_k_kernel(tc, hidden_states, Wk, bk, Wv, bv, out):
                 for i in range(length):
                     x_raw[g + i] = (x_tile, i)
             else:
-                w_tile = w_loads.tile([P, PACK, E], BF16)
+                w_tile = w_loads.tile([P, W_PIECE, PACK, E], BF16)
                 nc.sync.dma_start(
-                    out=w_tile[:].rearrange("p t n -> p (t n)"), in_=w_rows[m][:, g, :]
+                    out=w_tile[:].rearrange("p i t n -> p i (t n)"),
+                    in_=w_rows[m][:, g : g + W_PIECE, :],
                 )
-                w_raw[m, g] = w_tile
+                for i in range(W_PIECE):
+                    w_raw[m, g + i] = (w_tile, i)
 
         x_codes = keep.tile([P, PASSES, S], U32, align_bytes=64)
         x_scales = keep.tile([P, PASSES, S], U8, align_bytes=64)
@@ -139,7 +146,8 @@ def tile_linearattention_pa_k_kernel(tc, hidden_states, Wk, bk, Wv, bv, out):
 
         def regroup_w(m, g, vector_cols):
             w_grouped = w_stage.tile([P, E, PACK], BF16, align_bytes=64)
-            regroup(nc, w_grouped[:], w_raw[m, g][:], vector_cols)
+            w_tile, place = w_raw[m, g]
+            regroup(nc, w_grouped[:], w_tile[:, place], vector_cols)
             grouped["w", m, g] = w_grouped
 
         def quantise_item(item):

@@ -20,17 +20,21 @@ E = 512
 HEAD = 32
 PASSES = H // K_PASS
 ROW_TILES = S // P
+HALF = E // 2
 COL_TILES = E // P
 HEADS_PER_TILE = P // HEAD
 X_PIECES = (1, 1, 2, 2, 2, 2, 2, 2, 2)
-W_PIECE = 2
+W_PIECE = 1
 X_LEAD = 4
 GROUP = 2
-LOAD_LEAD = 9
+SPLIT = 2
+W_LEAD = 2
+LOAD_LEAD = 12
 RUN = 8
 MIXED_COLS = 304
-WEIGHT_COLS = 256
-LAST_COLS = 336
+WEIGHT_COLS = 240
+EPILOGUE_COLS = 304
+HALF_COLS = 112
 
 FLOPS = 2 * S * H * 2 * E + 2 * (E // HEAD) * HEAD * HEAD * S
 
@@ -54,7 +58,7 @@ def tile_linearattention_pa_k_kernel(tc, hidden_states, Wk, bk, Wv, bv, out):
         consts = stack.enter_context(tc.tile_pool(name="consts", bufs=1))
         keep = stack.enter_context(tc.tile_pool(name="keep", bufs=1))
         x_loads = stack.enter_context(tc.tile_pool(name="x_loads", bufs=6))
-        w_loads = stack.enter_context(tc.tile_pool(name="w_loads", bufs=7))
+        w_loads = stack.enter_context(tc.tile_pool(name="w_loads", bufs=12))
         x_stage = stack.enter_context(tc.tile_pool(name="x_stage", bufs=3))
         w_stage = stack.enter_context(tc.tile_pool(name="w_stage", bufs=4))
         psum_k = stack.enter_context(tc.psum_pool(name="psum_k", bufs=4))
@@ -67,12 +71,17 @@ def tile_linearattention_pa_k_kernel(tc, hidden_states, Wk, bk, Wv, bv, out):
         ident_cols = consts.tile([P, 2 * COL_TILES], BF16)
         nc.vector.tensor_copy(out=ident_cols[:], in_=ident[:, : 2 * COL_TILES])
 
-        items = [("x", 0, g) for g in range(X_LEAD)]
-        for g in range(0, PASSES, GROUP):
-            items += [("w", 0, i) for i in range(g, g + GROUP)]
-            items += [("x", 0, i) for i in range(g + X_LEAD, min(g + X_LEAD + GROUP, PASSES))]
+        items = [("x", 0, g, 0, S) for g in range(X_LEAD)]
+        items += [("w", 0, g, 0, E) for g in range(W_LEAD)]
+        for first in range(0, PASSES, GROUP):
+            x_passes = range(first + X_LEAD, min(first + X_LEAD + GROUP, PASSES))
+            w_passes = range(first + W_LEAD, min(first + W_LEAD + GROUP, PASSES))
+            items += [("x", 0, g, 0, S) for g in x_passes]
+            items += [("w", 0, g, 0, E) for g in w_passes]
         first_v = len(items)
-        items += [("w", 1, g) for g in range(PASSES)]
+        items += [("w", 1, g, 0, E) for g in range(PASSES - SPLIT)]
+        for lo in range(0, E, HALF):
+            items += [("w", 1, g, lo, lo + HALF) for g in range(PASSES - SPLIT, PASSES)]
 
         x_rows = hidden_states.flatten_outer_dims().rearrange("(r p) k -> p r k", p=P)
         w_rows = [w.rearrange("(g p t) n -> p g (t n)", p=P, t=PACK) for w in (Wk, Wv)]
@@ -83,14 +92,15 @@ def tile_linearattention_pa_k_kernel(tc, hidden_states, Wk, bk, Wv, bv, out):
         for length in X_PIECES:
             piece_at[first] = length
             first += length
-        loads = [
-            item
-            for item in items
-            if (item[0] == "w" and item[2] % W_PIECE == 0) or (item[0] == "x" and item[2] in piece_at)
-        ]
+        loads = []
+        for item in items:
+            if item[0] == "x" and item[2] in piece_at:
+                loads.append(item)
+            if item[0] == "w" and item[2] % W_PIECE == 0 and item[3] == 0:
+                loads.append(item)
 
         def load(item):
-            kind, m, g = item
+            kind, m, g = item[:3]
             if kind == "x":
                 length = piece_at[g]
                 x_tile = x_loads.tile([P, ROW_TILES, max(X_PIECES) * K_PASS], BF16)
@@ -139,31 +149,34 @@ def tile_linearattention_pa_k_kernel(tc, hidden_states, Wk, bk, Wv, bv, out):
                     nc.vector.tensor_copy(out=words_out, in_=words_in)
                 else:
                     nc.scalar.copy(out=words_out, in_=words_in)
-            grouped["x", 0, g] = x_grouped
+            return x_grouped
 
         sums = {}
         w_packed = {}
 
-        def regroup_w(m, g, vector_cols):
+        def regroup_w(m, g, lo, hi, vector_cols):
             w_grouped = w_stage.tile([P, E, PACK], BF16, align_bytes=64)
             w_tile, place = w_raw[m, g]
-            regroup(nc, w_grouped[:], w_tile[:, place], vector_cols)
-            grouped["w", m, g] = w_grouped
+            regroup(nc, w_grouped[:, lo:hi, :], w_tile[:, place, :, lo:hi], vector_cols)
+            return w_grouped
 
         def quantise_item(item):
-            kind, m, g = item
+            kind, m, g, lo, hi = item
             if kind == "x":
                 quantise(nc, grouped[item][:], x_codes[:, g, :], x_scales[:, g, :])
             else:
-                w_codes = w_stage.tile([P, E], U32, align_bytes=64)
-                w_scales = w_stage.tile([P, E], U8, align_bytes=64)
-                flat = grouped[item][:].rearrange("p n t -> p (n t)")
-                quantise(nc, flat, w_codes[:], w_scales[:])
-                w_packed[m, g] = (w_codes, w_scales)
+                if lo == 0:
+                    w_codes = w_stage.tile([P, E], U32, align_bytes=64)
+                    w_scales = w_stage.tile([P, E], U8, align_bytes=64)
+                    w_packed[m, g] = (w_codes, w_scales)
+                w_codes, w_scales = w_packed[m, g]
+                flat = grouped[item][:, lo:hi, :].rearrange("p n t -> p (n t)")
+                quantise(nc, flat, w_codes[:, lo:hi], w_scales[:, lo:hi])
 
-        def multiply(m, g):
+        def multiply(item):
+            kind, m, g, lo, hi = item
             w_codes, w_scales = w_packed[m, g]
-            for c in range(COL_TILES):
+            for c in range(lo // P, hi // P):
                 if g == 0:
                     pool = (psum_k, psum_x)[m]
                     sums[m, c] = pool.tile([P, S], F32, tag="bank", name="sums%d_%d" % (m, c))
@@ -240,28 +253,34 @@ def tile_linearattention_pa_k_kernel(tc, hidden_states, Wk, bk, Wv, bv, out):
         for item in loads[2:LOAD_LEAD]:
             load(item)
         issued = LOAD_LEAD
-        transpose_x(0)
+        for g in range(1):
+            transpose_x(g)
 
+        left_done = items.index(("w", 1, PASSES - 1, 0, HALF)) + 2
         for j in range(len(items) + 2):
             step = j - first_v
             if j + 1 < len(items) and items[j + 1][0] == "x":
                 transpose_x(items[j + 1][2])
             if j >= 2 and items[j - 2][0] == "w":
-                multiply(items[j - 2][1], items[j - 2][2])
+                multiply(items[j - 2])
             if step in (5, 6):
                 transpose_kv(0, 2 * (step - 5), 2)
-            if j == X_LEAD:
+            if j == 4:
                 spread_bias()
             if j < len(items):
-                kind, m, g = items[j]
+                kind, m, g, lo, hi = items[j]
                 if kind == "x":
-                    empty_x(g, g < X_LEAD)
-                elif m == 0:
-                    regroup_w(m, g, MIXED_COLS)
-                elif g == PASSES - 1:
-                    regroup_w(m, g, LAST_COLS)
+                    grouped[items[j]] = empty_x(g, False)
                 else:
-                    regroup_w(m, g, WEIGHT_COLS)
+                    if hi - lo < E:
+                        cols = HALF_COLS
+                    elif m == 0:
+                        cols = MIXED_COLS
+                    elif 2 <= step <= 8:
+                        cols = EPILOGUE_COLS
+                    else:
+                        cols = WEIGHT_COLS
+                    grouped[items[j]] = regroup_w(m, g, lo, hi, cols)
                 if items[j] in loads and issued < len(loads):
                     load(loads[issued])
                     issued += 1
@@ -271,34 +290,43 @@ def tile_linearattention_pa_k_kernel(tc, hidden_states, Wk, bk, Wv, bv, out):
                 empty_kv(0, 2 * (step - 7), 2, False)
             if 1 <= j <= len(items):
                 quantise_item(items[j - 1])
+            if j in (left_done, left_done + 1):
+                add_bias(1, j - left_done, False)
             if step == 9:
                 quantise_kv(0, 0, COL_TILES)
 
-        for c in range(COL_TILES):
-            add_bias(1, c, c % 2 == 1)
-        for c in range(COL_TILES):
-            transpose_kv(1, c, 1)
-        for c in range(COL_TILES):
-            empty_kv(1, c, 1, c % 2 == 1)
-            if c >= 1:
-                quantise_kv(1, c - 1, 1)
-        quantise_kv(1, COL_TILES - 1, 1)
-        products = psum_k.tile([P, COL_TILES, HEADS_PER_TILE, HEAD], F32, tag="bank")
-        for c in range(COL_TILES):
-            cols = slice(c * P, (c + 1) * P)
-            nc.tensor.matmul_mx(
-                out=products[:, c].rearrange("p r e -> p (r e)"),
-                lhsT=kv_codes[0][:, cols].bitcast(FP8X4),
-                lhsT_scale=kv_scales[0][:, cols],
-                rhs=kv_codes[1][:, cols].bitcast(FP8X4),
-                rhs_scale=kv_scales[1][:, cols],
-                start=True,
-                stop=True,
-            )
+        add_bias(1, 2, False)
+        add_bias(1, 3, True)
+        transpose_kv(1, 0, 2)
+        transpose_kv(1, 2, 1)
+        transpose_kv(1, 3, 1)
+        empty_kv(1, 0, 2, True)
+        empty_kv(1, 2, 1, False)
+        quantise_kv(1, 0, 2)
+        empty_kv(1, 3, 1, False)
+        quantise_kv(1, 2, 2)
         state = keep.tile([P, COL_TILES, HEAD], F32)
-        for r in range(HEADS_PER_TILE):
-            rows = slice(r * HEAD, (r + 1) * HEAD)
-            nc.vector.tensor_copy(out=state[rows, :, :], in_=products[rows, :, r, :])
+        for half in range(2):
+            tiles = COL_TILES // 2
+            products = psum_k.tile([P, tiles, HEADS_PER_TILE, HEAD], F32, tag="bank")
+            for i in range(tiles):
+                cols = slice((half * tiles + i) * P, (half * tiles + i + 1) * P)
+                nc.tensor.matmul_mx(
+                    out=products[:, i].rearrange("p r e -> p (r e)"),
+                    lhsT=kv_codes[0][:, cols].bitcast(FP8X4),
+                    lhsT_scale=kv_scales[0][:, cols],
+                    rhs=kv_codes[1][:, cols].bitcast(FP8X4),
+                    rhs_scale=kv_scales[1][:, cols],
+                    start=True,
+                    stop=True,
+                )
+            for r in range(HEADS_PER_TILE):
+                rows = slice(r * HEAD, (r + 1) * HEAD)
+                state_out = state[rows, half * tiles : (half + 1) * tiles, :]
+                if half == 0:
+                    nc.scalar.copy(out=state_out, in_=products[rows, :, r, :])
+                else:
+                    nc.vector.tensor_copy(out=state_out, in_=products[rows, :, r, :])
         nc.sync.dma_start(
             out=out.flatten_outer_dims().rearrange("(c p) e -> p c e", p=P), in_=state[:]
         )

@@ -25,14 +25,14 @@ COL_TILES = E // P
 HEADS_PER_TILE = P // HEAD
 X_PIECES = (1, 1, 2, 2, 2, 2, 2, 2, 2)
 W_PIECE = 1
-X_LEAD = 4
-GROUP = 2
+X_LEAD = 1
+GROUP = 1
 SPLIT = 2
-W_LEAD = 2
+W_LEAD = 1
 LOAD_LEAD = 12
 RUN = 8
-MIXED_COLS = 304
-WEIGHT_COLS = 240
+MIXED_COLS = 320
+WEIGHT_COLS = 256
 EPILOGUE_COLS = 304
 HALF_COLS = 112
 

from contextlib import ExitStack

import concourse.mybir as mybir
from concourse.masks import make_identity

F32 = mybir.dt.float32
BF16 = mybir.dt.bfloat16
U32 = mybir.dt.uint32
U8 = mybir.dt.uint8
FP8X4 = mybir.dt.float8_e4m3fn_x4
ADD = mybir.AluOpType.add
IDENTITY = mybir.ActivationFunctionType.Identity

P = 128
PACK = 4
K_PASS = P * PACK
S = 512
H = 8192
E = 512
HEAD = 32
PASSES = H // K_PASS
ROW_TILES = S // P
HALF = E // 2
COL_TILES = E // P
HEADS_PER_TILE = P // HEAD
X_PIECES = (1, 1, 2, 2, 2, 2, 2, 2, 2)
W_PIECE = 1
X_LEAD = 1
GROUP = 1
SPLIT = 2
W_LEAD = 1
LOAD_LEAD = 12
RUN = 8
MIXED_COLS = 320
WEIGHT_COLS = 256
EPILOGUE_COLS = 304
HALF_COLS = 112

FLOPS = 2 * S * H * 2 * E + 2 * (E // HEAD) * HEAD * HEAD * S


def regroup(nc, grouped, rows, vector_cols):
    dst = grouped.rearrange("p (c i) t -> p c t i", i=RUN)
    src = rows.rearrange("p t (c i) -> p c t i", i=RUN)
    cut = vector_cols // RUN
    nc.scalar.copy(out=dst[:, cut:], in_=src[:, cut:])
    nc.vector.tensor_copy(out=dst[:, :cut], in_=src[:, :cut])


def quantise(nc, grouped, codes, scales):
    nc.vector.quantize_mx(out=codes.bitcast(FP8X4), scales=scales, in_=grouped)


def tile_linearattention_pa_k_kernel(tc, hidden_states, Wk, bk, Wv, bv, out):
    nc = tc.nc
    with ExitStack() as stack:
        stack.enter_context(tc.manual_schedule())
        consts = stack.enter_context(tc.tile_pool(name="consts", bufs=1))
        keep = stack.enter_context(tc.tile_pool(name="keep", bufs=1))
        x_loads = stack.enter_context(tc.tile_pool(name="x_loads", bufs=6))
        w_loads = stack.enter_context(tc.tile_pool(name="w_loads", bufs=12))
        x_stage = stack.enter_context(tc.tile_pool(name="x_stage", bufs=3))
        w_stage = stack.enter_context(tc.tile_pool(name="w_stage", bufs=4))
        psum_k = stack.enter_context(tc.psum_pool(name="psum_k", bufs=4))
        psum_x = stack.enter_context(tc.psum_pool(name="psum_x", bufs=4))

        bias_rows = consts.tile([P, P], BF16)
        nc.vector.memset(bias_rows[:], 0.0)
        ident = consts.tile([P, P], F32)
        make_identity(nc, ident[:])
        ident_cols = consts.tile([P, 2 * COL_TILES], BF16)
        nc.vector.tensor_copy(out=ident_cols[:], in_=ident[:, : 2 * COL_TILES])

        items = [("x", 0, g, 0, S) for g in range(X_LEAD)]
        items += [("w", 0, g, 0, E) for g in range(W_LEAD)]
        for first in range(0, PASSES, GROUP):
            x_passes = range(first + X_LEAD, min(first + X_LEAD + GROUP, PASSES))
            w_passes = range(first + W_LEAD, min(first + W_LEAD + GROUP, PASSES))
            items += [("x", 0, g, 0, S) for g in x_passes]
            items += [("w", 0, g, 0, E) for g in w_passes]
        first_v = len(items)
        items += [("w", 1, g, 0, E) for g in range(PASSES - SPLIT)]
        for lo in range(0, E, HALF):
            items += [("w", 1, g, lo, lo + HALF) for g in range(PASSES - SPLIT, PASSES)]

        x_rows = hidden_states.flatten_outer_dims().rearrange("(r p) k -> p r k", p=P)
        w_rows = [w.rearrange("(g p t) n -> p g (t n)", p=P, t=PACK) for w in (Wk, Wv)]
        x_raw = {}
        w_raw = {}
        piece_at = {}
        first = 0
        for length in X_PIECES:
            piece_at[first] = length
            first += length
        loads = []
        for item in items:
            if item[0] == "x" and item[2] in piece_at:
                loads.append(item)
            if item[0] == "w" and item[2] % W_PIECE == 0 and item[3] == 0:
                loads.append(item)

        def load(item):
            kind, m, g = item[:3]
            if kind == "x":
                length = piece_at[g]
                x_tile = x_loads.tile([P, ROW_TILES, max(X_PIECES) * K_PASS], BF16)
                nc.sync.dma_start(
                    out=x_tile[:, :, : length * K_PASS],
                    in_=x_rows[:, :, g * K_PASS : (g + length) * K_PASS],
                )
                for i in range(length):
                    x_raw[g + i] = (x_tile, i)
            else:
                w_tile = w_loads.tile([P, W_PIECE, PACK, E], BF16)
                nc.sync.dma_start(
                    out=w_tile[:].rearrange("p i t n -> p i (t n)"),
                    in_=w_rows[m][:, g : g + W_PIECE, :],
                )
                for i in range(W_PIECE):
                    w_raw[m, g + i] = (w_tile, i)

        x_codes = keep.tile([P, PASSES, S], U32, align_bytes=64)
        x_scales = keep.tile([P, PASSES, S], U8, align_bytes=64)
        x_banks = {}
        grouped = {}

        def transpose_x(g):
            x_tile, place = x_raw[g]
            words_per_pass = K_PASS // 2
            for half in range(2):
                xt = psum_x.tile([P, 2, 2, P], F32, tag="bank")
                for r in range(2):
                    words = x_tile[:, 2 * half + r, :].bitcast(F32)
                    for u in range(2):
                        nc.tensor.transpose(
                            xt[:, r, u, :],
                            words[:, place * words_per_pass + u : (place + 1) * words_per_pass : 2],
                            ident[:],
                        )
                x_banks[g, half] = xt

        def empty_x(g, share):
            x_grouped = x_stage.tile([P, S * PACK], BF16, align_bytes=64)
            words = x_grouped[:].bitcast(F32).rearrange("p (r s u) -> p r s u", r=ROW_TILES, u=2)
            for half in range(2):
                words_out = words[:, 2 * half : 2 * half + 2]
                words_in = x_banks[g, half][:].rearrange("p r u s -> p r s u")
                if half == 1 and share:
                    nc.vector.tensor_copy(out=words_out, in_=words_in)
                else:
                    nc.scalar.copy(out=words_out, in_=words_in)
            return x_grouped

        sums = {}
        w_packed = {}

        def regroup_w(m, g, lo, hi, vector_cols):
            w_grouped = w_stage.tile([P, E, PACK], BF16, align_bytes=64)
            w_tile, place = w_raw[m, g]
            regroup(nc, w_grouped[:, lo:hi, :], w_tile[:, place, :, lo:hi], vector_cols)
            return w_grouped

        def quantise_item(item):
            kind, m, g, lo, hi = item
            if kind == "x":
                quantise(nc, grouped[item][:], x_codes[:, g, :], x_scales[:, g, :])
            else:
                if lo == 0:
                    w_codes = w_stage.tile([P, E], U32, align_bytes=64)
                    w_scales = w_stage.tile([P, E], U8, align_bytes=64)
                    w_packed[m, g] = (w_codes, w_scales)
                w_codes, w_scales = w_packed[m, g]
                flat = grouped[item][:, lo:hi, :].rearrange("p n t -> p (n t)")
                quantise(nc, flat, w_codes[:, lo:hi], w_scales[:, lo:hi])

        def multiply(item):
            kind, m, g, lo, hi = item
            w_codes, w_scales = w_packed[m, g]
            for c in range(lo // P, hi // P):
                if g == 0:
                    pool = (psum_k, psum_x)[m]
                    sums[m, c] = pool.tile([P, S], F32, tag="bank", name="sums%d_%d" % (m, c))
                cols = slice(c * P, (c + 1) * P)
                nc.tensor.matmul_mx(
                    out=sums[m, c][:],
                    lhsT=w_codes[:, cols].bitcast(FP8X4),
                    lhsT_scale=w_scales[:, cols],
                    rhs=x_codes[:, g, :].bitcast(FP8X4),
                    rhs_scale=x_scales[:, g, :],
                    start=(g == 0),
                    stop=(g == PASSES - 1),
                )

        bias = consts.tile([P, 2 * COL_TILES], F32)
        rounded = [keep.tile([P, COL_TILES, S], BF16, name="rounded%d" % m) for m in range(2)]
        kv_grouped = [
            keep.tile([P, COL_TILES, P * PACK], BF16, name="kv_grouped%d" % m, align_bytes=64)
            for m in range(2)
        ]
        kv_codes = [keep.tile([P, E], U32, name="kv_codes%d" % m, align_bytes=64) for m in range(2)]
        kv_scales = [keep.tile([P, E], U8, name="kv_scales%d" % m, align_bytes=64) for m in range(2)]
        kv_banks = {}

        def spread_bias():
            columns = psum_x.tile([P, 2 * COL_TILES], F32, tag="bank")
            nc.tensor.matmul(
                out=columns[:], lhsT=bias_rows[:], rhs=ident_cols[:], start=True, stop=True
            )
            nc.vector.tensor_copy(out=bias[:], in_=columns[:])

        def add_bias(m, c, on_vector):
            column = bias[:, m * COL_TILES + c : m * COL_TILES + c + 1]
            if on_vector:
                nc.vector.tensor_scalar(
                    out=rounded[m][:, c, :], in0=sums[m, c][:], scalar1=column, scalar2=None, op0=ADD
                )
            else:
                nc.scalar.activation(
                    out=rounded[m][:, c, :], in_=sums[m, c][:], func=IDENTITY, bias=column, scale=1.0
                )

        def transpose_kv(m, first_c, tiles):
            turned = psum_k.tile([P, tiles, 2, P], F32, tag="bank")
            for c in range(tiles):
                words = rounded[m][:, first_c + c, :].bitcast(F32)
                for u in range(2):
                    nc.tensor.transpose(turned[:, c, u, :], words[:, u::2], ident[:])
            kv_banks[m, first_c] = turned

        def empty_kv(m, first_c, tiles, on_vector):
            cols = slice(first_c, first_c + tiles)
            words_out = kv_grouped[m][:, cols, :].bitcast(F32).rearrange(
                "p c (n u) -> p c n u", u=2
            )
            words_in = kv_banks[m, first_c][:].rearrange("p c u n -> p c n u")
            if on_vector:
                nc.vector.tensor_copy(out=words_out, in_=words_in)
            else:
                nc.scalar.copy(out=words_out, in_=words_in)

        def quantise_kv(m, first_c, tiles):
            cols = slice(first_c * P, (first_c + tiles) * P)
            flat = kv_grouped[m][:, first_c : first_c + tiles, :].rearrange("p c i -> p (c i)")
            quantise(nc, flat, kv_codes[m][:, cols], kv_scales[m][:, cols])

        for item in loads[:2]:
            load(item)
        for m, b in enumerate((bk, bv)):
            nc.sync.dma_start(
                out=bias_rows[m * COL_TILES : (m + 1) * COL_TILES, :],
                in_=b.rearrange("(c p) -> c p", p=P),
            )
        for item in loads[2:LOAD_LEAD]:
            load(item)
        issued = LOAD_LEAD
        for g in range(1):
            transpose_x(g)

        left_done = items.index(("w", 1, PASSES - 1, 0, HALF)) + 2
        for j in range(len(items) + 2):
            step = j - first_v
            if j + 1 < len(items) and items[j + 1][0] == "x":
                transpose_x(items[j + 1][2])
            if j >= 2 and items[j - 2][0] == "w":
                multiply(items[j - 2])
            if step in (5, 6):
                transpose_kv(0, 2 * (step - 5), 2)
            if j == 4:
                spread_bias()
            if j < len(items):
                kind, m, g, lo, hi = items[j]
                if kind == "x":
                    grouped[items[j]] = empty_x(g, False)
                else:
                    if hi - lo < E:
                        cols = HALF_COLS
                    elif m == 0:
                        cols = MIXED_COLS
                    elif 2 <= step <= 8:
                        cols = EPILOGUE_COLS
                    else:
                        cols = WEIGHT_COLS
                    grouped[items[j]] = regroup_w(m, g, lo, hi, cols)
                if items[j] in loads and issued < len(loads):
                    load(loads[issued])
                    issued += 1
            if 2 <= step < 2 + COL_TILES:
                add_bias(0, step - 2, False)
            if step in (7, 8):
                empty_kv(0, 2 * (step - 7), 2, False)
            if 1 <= j <= len(items):
                quantise_item(items[j - 1])
            if j in (left_done, left_done + 1):
                add_bias(1, j - left_done, False)
            if step == 9:
                quantise_kv(0, 0, COL_TILES)

        add_bias(1, 2, False)
        add_bias(1, 3, True)
        transpose_kv(1, 0, 2)
        transpose_kv(1, 2, 1)
        transpose_kv(1, 3, 1)
        empty_kv(1, 0, 2, True)
        empty_kv(1, 2, 1, False)
        quantise_kv(1, 0, 2)
        empty_kv(1, 3, 1, False)
        quantise_kv(1, 2, 2)
        state = keep.tile([P, COL_TILES, HEAD], F32)
        for half in range(2):
            tiles = COL_TILES // 2
            products = psum_k.tile([P, tiles, HEADS_PER_TILE, HEAD], F32, tag="bank")
            for i in range(tiles):
                cols = slice((half * tiles + i) * P, (half * tiles + i + 1) * P)
                nc.tensor.matmul_mx(
                    out=products[:, i].rearrange("p r e -> p (r e)"),
                    lhsT=kv_codes[0][:, cols].bitcast(FP8X4),
                    lhsT_scale=kv_scales[0][:, cols],
                    rhs=kv_codes[1][:, cols].bitcast(FP8X4),
                    rhs_scale=kv_scales[1][:, cols],
                    start=True,
                    stop=True,
                )
            for r in range(HEADS_PER_TILE):
                rows = slice(r * HEAD, (r + 1) * HEAD)
                state_out = state[rows, half * tiles : (half + 1) * tiles, :]
                if half == 0:
                    nc.scalar.copy(out=state_out, in_=products[rows, :, r, :])
                else:
                    nc.vector.tensor_copy(out=state_out, in_=products[rows, :, r, :])
        nc.sync.dma_start(
            out=out.flatten_outer_dims().rearrange("(c p) e -> p c e", p=P), in_=state[:]
        )
